import numpy as np
import ml_dtypes


def mxq(x, axis, fmt="e4m3"):
    dtype, down = {"e4m3": (ml_dtypes.float8_e4m3fn, 7), "e5m2": (ml_dtypes.float8_e5m2, 14)}[fmt]
    v = np.moveaxis(np.asarray(x, np.float32).astype(ml_dtypes.bfloat16).astype(np.float64), axis, -1)
    blocks = v.reshape(v.shape[:-1] + (-1, 32))
    amax = np.abs(blocks).max(-1, keepdims=True)
    byte = np.maximum(np.where(amax > 0, np.frexp(amax)[1] - 1 + 127, 0) - down, 1)
    scale = np.exp2(byte - 127.0)
    codes = (blocks / scale).astype(np.float32).astype(dtype).astype(np.float64)
    return np.moveaxis((codes * scale).reshape(v.shape), -1, axis)


WIDE = False


def mx_kscale(k):
    if not WIDE:
        return np.ones(k)
    levels = np.array([10, -10, 5, -5, 0])
    if k % 512:
        return np.exp2(np.random.permutation(np.resize(levels, k // 32))).repeat(32)
    a = np.empty((k // 512, 16))
    for p in range(k // 512):
        a[p, :8] = np.random.permutation(np.resize(levels, 8))
        for g in range(8):
            far = levels[np.abs(levels - a[p, g]) >= 10]
            a[p, g + 8] = far[np.random.randint(len(far))]
    return np.exp2(a.ravel()).repeat(32)


BF16 = ml_dtypes.bfloat16


def bf(x):
    return np.asarray(x, np.float32).astype(BF16)


def f64(x):
    return np.asarray(x).astype(np.float64)


B, N, HD, NH, KVH, D = 8, 512, 512, 8, 2, 128
QD = NH * D
KVD = KVH * D
EPS = 2.0 ** -23


def setup_inputs():
    s = mx_kscale(HD)
    rows = np.exp2(np.random.uniform(-2.0, 2.0, (B, N, 1)))
    rows = np.where(np.random.random((B, N, 1)) < 0.125, rows * 2.0 ** -11, rows)
    return {"tokens": bf(np.random.standard_normal((B, N, HD)) * rows),
            "norm_w": bf((1.0 + 0.1 * np.random.standard_normal(HD)) * s),
            "Wq": bf(np.random.standard_normal((QD, HD)) * 0.4 / np.sqrt(HD) / s[None, :]),
            "bq": bf(np.random.standard_normal(QD) * 0.1),
            "Wk": bf(np.random.standard_normal((KVD, HD)) * 0.4 / np.sqrt(HD) / s[None, :]),
            "bk": bf(np.random.standard_normal(KVD) * 0.1),
            "Wv": bf(np.random.standard_normal((KVD, HD)) / np.sqrt(HD) / s[None, :]),
            "bv": bf(np.random.standard_normal(KVD) * 0.3)}


def reference(tokens, norm_w, Wq, bq, Wk, bk, Wv, bv):
    t = f64(tokens)
    x = t / np.sqrt(np.mean(t * t, axis=-1, keepdims=True) + EPS) * f64(norm_w)
    xq = mxq(x, 2, "e4m3")
    q = ((xq @ mxq(f64(Wq), 1, "e4m3").T) + f64(bq)).reshape(B, N, NH, D).transpose(0, 2, 1, 3)
    k = ((xq @ mxq(f64(Wk), 1, "e4m3").T) + f64(bk)).reshape(B, N, KVH, D).transpose(0, 2, 1, 3)
    v = ((xq @ mxq(f64(Wv), 1, "e4m3").T) + f64(bv)).reshape(B, N, KVH, D).transpose(0, 2, 1, 3)
    return q, k, v

@@ -1,0 +1,279 @@
+from contextlib import ExitStack
+
+import concourse.masks as masks
+import concourse.mybir as mybir
+
+F32 = mybir.dt.float32
+BF16 = mybir.dt.bfloat16
+U32 = mybir.dt.uint32
+U8 = mybir.dt.uint8
+FP8X4 = mybir.dt.float8_e4m3fn_x4
+ACT = mybir.ActivationFunctionType
+ALU = mybir.AluOpType
+
+P = 128
+BATCHES = 8
+TOKENS = 512
+HIDDEN = 512
+HEAD = 128
+Q_HEADS = 8
+KV_HEADS = 2
+EPS = 2.0**-23
+
+TILES = TOKENS // P
+PACK = 4
+HALVES = 2
+GROUP_HEADS = 4
+GROUP = GROUP_HEADS * HEAD
+COLUMNS = (Q_HEADS + 2 * KV_HEADS) * HEAD
+GROUPS = COLUMNS // GROUP
+Q_GROUPS = Q_HEADS // GROUP_HEADS
+QUANT = TILES * P * PACK
+GAIN_AHEAD = 2
+SCALAR_GROUPS = 2
+
+FLOPS = 2 * BATCHES * TOKENS * HIDDEN * COLUMNS
+
+
+def tile_attentionlayerdecoder_pa_t_kernel(
+    tc, tokens, norm_w, Wq, bq, Wk, bk, Wv, bv, q_out, k_out, v_out
+):
+    nc = tc.nc
+    with ExitStack() as ctx:
+        ctx.enter_context(tc.manual_schedule())
+        const = ctx.enter_context(tc.tile_pool(name="const", bufs=1))
+        stats = ctx.enter_context(tc.tile_pool(name="stats", bufs=3))
+        squares = ctx.enter_context(tc.tile_pool(name="squares", bufs=4))
+        gained = ctx.enter_context(tc.tile_pool(name="gained", bufs=GAIN_AHEAD + 1))
+        normed = ctx.enter_context(tc.tile_pool(name="normed", bufs=2))
+        packed = ctx.enter_context(tc.tile_pool(name="packed", bufs=2))
+        results = ctx.enter_context(tc.tile_pool(name="results", bufs=6))
+        flipped = ctx.enter_context(tc.psum_pool(name="flipped", bufs=3))
+        sums = ctx.enter_context(tc.psum_pool(name="sums", bufs=5))
+
+        eps = const.tile([P, 1], F32)
+        nc.vector.memset(eps[:], EPS)
+        gain_row = const.tile([P, HIDDEN], BF16)
+        nc.vector.memset(gain_row[:], 0.0)
+        bias_row = const.tile([P, COLUMNS], BF16)
+        nc.vector.memset(bias_row[:], 0.0)
+        ones = const.tile([P, P], BF16)
+        nc.vector.memset(ones[:], 1.0)
+        ident = const.tile([P, P], F32)
+        masks.make_identity(nc, ident[:])
+        table_warm = const.tile([P, 1], F32)
+        nc.scalar.activation(out=table_warm[:], in_=eps[:], func=ACT.Abs_reciprocal_sqrt)
+
+        token_tiles = {}
+
+        def load_tokens(b):
+            token_tiles[b] = const.tile([P, TILES, HIDDEN], BF16, name="tokens%d" % b)
+            nc.sync.dma_start(
+                out=token_tiles[b][:], in_=tokens[b].rearrange("(p j) k -> p j k", j=TILES)
+            )
+
+        w_raw = const.tile([P, COLUMNS // P * HIDDEN], BF16)
+        w_rows = w_raw[:].rearrange("p (r k) -> p r k", k=HIDDEN)
+
+        def load_weight_rows(first_tile, rows):
+            n_tiles = rows.shape[0] // P
+            nc.sync.dma_start(
+                out=w_rows[:, first_tile : first_tile + n_tiles, :],
+                in_=rows.rearrange("(r p) k -> p r k", p=P),
+            )
+
+        q_columns = Q_HEADS * HEAD
+        kv_columns = KV_HEADS * HEAD
+        load_tokens(0)
+        nc.sync.dma_start(out=gain_row[0:1, :], in_=norm_w.unsqueeze(0))
+        load_tokens(1)
+        for g in range(Q_GROUPS):
+            load_weight_rows(g * GROUP_HEADS, Wq[g * GROUP : (g + 1) * GROUP, :])
+        load_weight_rows(Q_HEADS, Wk)
+        load_weight_rows(Q_HEADS + KV_HEADS, Wv)
+        nc.sync.dma_start(out=bias_row[0:1, 0:q_columns], in_=bq.unsqueeze(0))
+        nc.sync.dma_start(out=bias_row[0:1, q_columns : q_columns + kv_columns], in_=bk.unsqueeze(0))
+        nc.sync.dma_start(out=bias_row[0:1, q_columns + kv_columns : COLUMNS], in_=bv.unsqueeze(0))
+        for b in range(2, BATCHES):
+            load_tokens(b)
+
+        def repeat_row(row, out):
+            spread = sums.tile([P, GROUP], F32, name="acc")
+            nc.tensor.matmul(out=spread[:], lhsT=ones[:], rhs=row, start=True, stop=True)
+            nc.vector.tensor_copy(out=out, in_=spread[:])
+
+        gain = const.tile([P, HIDDEN], BF16)
+        bias = const.tile([P, COLUMNS], F32)
+
+        inverse_root, gained_tokens, x_codes, x_scales = {}, {}, {}, {}
+
+        def apply_gain(b, half):
+            if half == 0:
+                gained_tokens[b] = gained.tile([P, TILES, HIDDEN], F32, name="gained_tokens")
+            two = slice(2 * half, 2 * half + 2)
+            nc.gpsimd.tensor_tensor(
+                out=gained_tokens[b][:, two, :],
+                in0=token_tiles[b][:, two, :],
+                in1=gain[:].unsqueeze(1).to_broadcast([P, 2, HIDDEN]),
+                op=ALU.mult,
+            )
+
+        def take_stats(b):
+            square_sum = stats.tile([P, TILES], F32, name="square_sum")
+            for j in range(TILES):
+                unread = squares.tile([P, HIDDEN], BF16, name="unread")
+                nc.scalar.activation(
+                    out=unread[:],
+                    in_=token_tiles[b][:, j, :],
+                    func=ACT.Square,
+                    accum_out=square_sum[:, j : j + 1],
+                )
+            inverse_root[b] = stats.tile([P, TILES], F32, name="inverse_root")
+            nc.scalar.activation(
+                out=inverse_root[b][:],
+                in_=square_sum[:],
+                func=ACT.Abs_reciprocal_sqrt,
+                bias=eps[:],
+                scale=1.0 / HIDDEN,
+            )
+
+        def normalise(b):
+            x = normed.tile([P, TILES * HIDDEN], BF16, name="x")
+            for j in range(TILES):
+                nc.scalar.activation(
+                    out=x[:, j * HIDDEN : (j + 1) * HIDDEN],
+                    in_=gained_tokens[b][:, j, :],
+                    func=ACT.Copy,
+                    scale=inverse_root[b][:, j : j + 1],
+                )
+            return x
+
+        def k_to_partitions(row_words, grouped_words, copy):
+            for pair in range(TILES // 2):
+                flip = flipped.tile([P, 2, HALVES, P], F32, name="flip")
+                for i in range(2):
+                    for u in range(HALVES):
+                        nc.tensor.transpose(
+                            out=flip[:, i, u, :],
+                            in_=row_words[:, 2 * pair + i, u : HALVES * P : HALVES],
+                            identity=ident[:],
+                        )
+                copy(
+                    out=grouped_words[:, 2 * pair : 2 * pair + 2, :, :],
+                    in_=flip[:].rearrange("p i u n -> p i n u"),
+                )
+
+        def as_row_words(tile_2d):
+            return tile_2d.bitcast(F32).rearrange("p (i w) -> p i w", i=TILES)
+
+        def as_grouped_words(tile_2d):
+            return tile_2d.bitcast(F32).rearrange("p (i n u) -> p i n u", i=TILES, u=HALVES)
+
+        def flip_x(x):
+            grouped = normed.tile([P, QUANT], BF16, name="grouped", align_bytes=64)
+            k_to_partitions(as_row_words(x[:]), as_grouped_words(grouped[:]), nc.scalar.copy)
+            return grouped
+
+        def quantise_x(b, grouped):
+            x_codes[b] = packed.tile([P, TILES * P], U32, name="x_codes", align_bytes=64)
+            x_scales[b] = packed.tile([P, TILES * P], U8, name="x_scales", align_bytes=64)
+            nc.vector.quantize_mx(
+                out=x_codes[b][:].bitcast(FP8X4), scales=x_scales[b][:], in_=grouped[:]
+            )
+
+        w_grouped = const.tile([P, GROUPS * QUANT], BF16, align_bytes=64)
+        w_codes = const.tile([P, COLUMNS], U32, align_bytes=64)
+        w_scales = const.tile([P, COLUMNS], U8, align_bytes=64)
+
+        def pack_weights(g):
+            k_to_partitions(
+                as_row_words(w_raw[:, g * GROUP_HEADS * HIDDEN : (g + 1) * GROUP_HEADS * HIDDEN]),
+                as_grouped_words(w_grouped[:, g * QUANT : (g + 1) * QUANT]),
+                nc.vector.tensor_copy,
+            )
+            nc.vector.quantize_mx(
+                out=w_codes[:, g * GROUP : (g + 1) * GROUP].bitcast(FP8X4),
+                scales=w_scales[:, g * GROUP : (g + 1) * GROUP],
+                in_=w_grouped[:, g * QUANT : (g + 1) * QUANT],
+            )
+
+        def by_head(columns):
+            return columns.rearrange("p (h d) -> p h d", d=HEAD)
+
+        def multiply(b, g):
+            columns = slice(g * GROUP, (g + 1) * GROUP)
+            banks = []
+            for j in range(TILES):
+                rows = slice(j * P, (j + 1) * P)
+                acc = sums.tile([P, GROUP], F32, name="acc")
+                nc.tensor.matmul_mx(
+                    out=acc[:],
+                    lhsT=x_codes[b][:, rows].bitcast(FP8X4),
+                    lhsT_scale=x_scales[b][:, rows],
+                    rhs=w_codes[:, columns].bitcast(FP8X4),
+                    rhs_scale=w_scales[:, columns],
+                    start=True,
+                    stop=True,
+                )
+                banks.append(acc)
+            return banks
+
+        def store(heads_out, y_heads):
+            nc.sync.dma_start(
+                out=heads_out.rearrange("h (p j) d -> p h (j d)", j=TILES),
+                in_=y_heads.rearrange("p h j d -> p h (j d)"),
+            )
+
+        def add_bias_and_store(b, g, banks):
+            columns = slice(g * GROUP, (g + 1) * GROUP)
+            y = results.tile([P, GROUP_HEADS, TILES, HEAD], F32, name="y")
+            for j in range(TILES):
+                if j == 0 and g < SCALAR_GROUPS:
+                    nc.scalar.copy(out=y[:, :, j, :], in_=by_head(banks[j][:]))
+                    nc.gpsimd.tensor_tensor(
+                        out=y[:, :, j, :], in0=y[:, :, j, :], in1=by_head(bias[:, columns]), op=ALU.add
+                    )
+                else:
+                    nc.vector.tensor_tensor(
+                        out=y[:, :, j, :],
+                        in0=by_head(banks[j][:]),
+                        in1=by_head(bias[:, columns]),
+                        op=ALU.add,
+                    )
+            if g < Q_GROUPS:
+                store(q_out[b, g * GROUP_HEADS : (g + 1) * GROUP_HEADS], y[:])
+            else:
+                store(k_out[b], y[:, 0:KV_HEADS])
+                store(v_out[b], y[:, KV_HEADS : 2 * KV_HEADS])
+
+        repeat_row(gain_row[:], gain[:])
+        for b in range(GAIN_AHEAD):
+            apply_gain(b, 0)
+            apply_gain(b, 1)
+        take_stats(0)
+        for g in range(GROUPS):
+            pack_weights(g)
+        for g in range(GROUPS):
+            repeat_row(bias_row[:, g * GROUP : (g + 1) * GROUP], bias[:, g * GROUP : (g + 1) * GROUP])
+        quantise_x(0, flip_x(normalise(0)))
+        take_stats(1)
+
+        for b in range(BATCHES):
+            following = b + 1 < BATCHES
+            gain_due = b + GAIN_AHEAD < BATCHES
+            add_bias_and_store(b, 0, multiply(b, 0))
+            if gain_due:
+                apply_gain(b + GAIN_AHEAD, 0)
+            if following:
+                x_next = normalise(b + 1)
+            banks = multiply(b, 1)
+            if following:
+                grouped_next = flip_x(x_next)
+            add_bias_and_store(b, 1, banks)
+            if gain_due:
+                apply_gain(b + GAIN_AHEAD, 1)
+            if following:
+                quantise_x(b + 1, grouped_next)
+            if b + 2 < BATCHES:
+                take_stats(b + 2)
+            add_bias_and_store(b, 2, multiply(b, 2))

@@ -29,8 +29,7 @@ COLUMNS = (Q_HEADS + 2 * KV_HEADS) * HEAD
 GROUPS = COLUMNS // GROUP
 Q_GROUPS = Q_HEADS // GROUP_HEADS
 QUANT = TILES * P * PACK
-GAIN_AHEAD = 2
-SCALAR_GROUPS = 2
+PASSES = GROUPS * TILES
 
 FLOPS = 2 * BATCHES * TOKENS * HIDDEN * COLUMNS
 
@@ -44,33 +43,39 @@ def tile_attentionlayerdecoder_pa_t_kernel(
         const = ctx.enter_context(tc.tile_pool(name="const", bufs=1))
         stats = ctx.enter_context(tc.tile_pool(name="stats", bufs=3))
         squares = ctx.enter_context(tc.tile_pool(name="squares", bufs=4))
-        gained = ctx.enter_context(tc.tile_pool(name="gained", bufs=GAIN_AHEAD + 1))
         normed = ctx.enter_context(tc.tile_pool(name="normed", bufs=2))
         packed = ctx.enter_context(tc.tile_pool(name="packed", bufs=2))
-        results = ctx.enter_context(tc.tile_pool(name="results", bufs=6))
-        flipped = ctx.enter_context(tc.psum_pool(name="flipped", bufs=3))
+        results = ctx.enter_context(tc.tile_pool(name="results", bufs=12))
+        fixed = ctx.enter_context(tc.psum_pool(name="fixed", bufs=1))
+        flipped = ctx.enter_context(tc.psum_pool(name="flipped", bufs=2))
         sums = ctx.enter_context(tc.psum_pool(name="sums", bufs=5))
 
         eps = const.tile([P, 1], F32)
         nc.vector.memset(eps[:], EPS)
         gain_row = const.tile([P, HIDDEN], BF16)
         nc.vector.memset(gain_row[:], 0.0)
-        bias_row = const.tile([P, COLUMNS], BF16)
-        nc.vector.memset(bias_row[:], 0.0)
         ones = const.tile([P, P], BF16)
         nc.vector.memset(ones[:], 1.0)
         ident = const.tile([P, P], F32)
         masks.make_identity(nc, ident[:])
+        bias_row = const.tile([P, COLUMNS], BF16)
+        nc.vector.memset(bias_row[:], 0.0)
         table_warm = const.tile([P, 1], F32)
         nc.scalar.activation(out=table_warm[:], in_=eps[:], func=ACT.Abs_reciprocal_sqrt)
 
         token_tiles = {}
 
-        def load_tokens(b):
+        def load_tokens(b, pieces=1):
             token_tiles[b] = const.tile([P, TILES, HIDDEN], BF16, name="tokens%d" % b)
-            nc.sync.dma_start(
-                out=token_tiles[b][:], in_=tokens[b].rearrange("(p j) k -> p j k", j=TILES)
-            )
+            rows = tokens[b].rearrange("(p j) k -> p j k", j=TILES)
+            width = TILES // pieces
+            return [
+                (token_tiles[b][:, i * width : (i + 1) * width, :], rows[:, i * width : (i + 1) * width, :])
+                for i in range(pieces)
+            ]
+
+        def load(piece):
+            nc.sync.dma_start(out=piece[0], in_=piece[1])
 
         w_raw = const.tile([P, COLUMNS // P * HIDDEN], BF16)
         w_rows = w_raw[:].rearrange("p (r k) -> p r k", k=HIDDEN)
@@ -84,113 +89,108 @@ def tile_attentionlayerdecoder_pa_t_kernel(
 
         q_columns = Q_HEADS * HEAD
         kv_columns = KV_HEADS * HEAD
-        load_tokens(0)
+        first_half, second_half = load_tokens(0, pieces=2)
         nc.sync.dma_start(out=gain_row[0:1, :], in_=norm_w.unsqueeze(0))
-        load_tokens(1)
-        for g in range(Q_GROUPS):
-            load_weight_rows(g * GROUP_HEADS, Wq[g * GROUP : (g + 1) * GROUP, :])
-        load_weight_rows(Q_HEADS, Wk)
-        load_weight_rows(Q_HEADS + KV_HEADS, Wv)
+        load(first_half)
+        load(second_half)
+        load_weight_rows(0, Wq[0:GROUP, :])
         nc.sync.dma_start(out=bias_row[0:1, 0:q_columns], in_=bq.unsqueeze(0))
         nc.sync.dma_start(out=bias_row[0:1, q_columns : q_columns + kv_columns], in_=bk.unsqueeze(0))
         nc.sync.dma_start(out=bias_row[0:1, q_columns + kv_columns : COLUMNS], in_=bv.unsqueeze(0))
+        load_weight_rows(GROUP_HEADS, Wq[GROUP : 2 * GROUP, :])
+        load(load_tokens(1)[0])
+        load_weight_rows(Q_HEADS, Wk)
+        load_weight_rows(Q_HEADS + KV_HEADS, Wv)
         for b in range(2, BATCHES):
-            load_tokens(b)
+            load(load_tokens(b)[0])
 
-        def repeat_row(row, out):
-            spread = sums.tile([P, GROUP], F32, name="acc")
-            nc.tensor.matmul(out=spread[:], lhsT=ones[:], rhs=row, start=True, stop=True)
-            nc.vector.tensor_copy(out=out, in_=spread[:])
-
-        gain = const.tile([P, HIDDEN], BF16)
+        gain = fixed.tile([P, HIDDEN], F32)
+        nc.tensor.matmul(out=gain[:], lhsT=ones[:], rhs=gain_row[:], start=True, stop=True)
         bias = const.tile([P, COLUMNS], F32)
 
-        inverse_root, gained_tokens, x_codes, x_scales = {}, {}, {}, {}
+        def repeat_bias(g, copy):
+            columns = slice(g * GROUP, (g + 1) * GROUP)
+            spread = sums.tile([P, GROUP], F32, name="acc")
+            nc.tensor.matmul(out=spread[:], lhsT=ones[:], rhs=bias_row[:, columns], start=True, stop=True)
+            copy(out=bias[:, columns], in_=spread[:])
 
-        def apply_gain(b, half):
-            if half == 0:
-                gained_tokens[b] = gained.tile([P, TILES, HIDDEN], F32, name="gained_tokens")
-            two = slice(2 * half, 2 * half + 2)
-            nc.gpsimd.tensor_tensor(
-                out=gained_tokens[b][:, two, :],
-                in0=token_tiles[b][:, two, :],
-                in1=gain[:].unsqueeze(1).to_broadcast([P, 2, HIDDEN]),
-                op=ALU.mult,
+        square_sum, inverse_root, x_rows, x_grouped = {}, {}, {}, {}
+        x_codes, x_scales, results_of = {}, {}, {}
+
+        def square(b, j):
+            if j == 0:
+                square_sum[b] = stats.tile([P, TILES], F32, name="square_sum")
+                inverse_root[b] = stats.tile([P, TILES], F32, name="inverse_root")
+            unread = squares.tile([P, HIDDEN], BF16, name="unread")
+            nc.scalar.activation(
+                out=unread[:],
+                in_=token_tiles[b][:, j, :],
+                func=ACT.Square,
+                accum_out=square_sum[b][:, j : j + 1],
             )
 
-        def take_stats(b):
-            square_sum = stats.tile([P, TILES], F32, name="square_sum")
-            for j in range(TILES):
-                unread = squares.tile([P, HIDDEN], BF16, name="unread")
-                nc.scalar.activation(
-                    out=unread[:],
-                    in_=token_tiles[b][:, j, :],
-                    func=ACT.Square,
-                    accum_out=square_sum[:, j : j + 1],
-                )
-            inverse_root[b] = stats.tile([P, TILES], F32, name="inverse_root")
+        def root(b, tiles=slice(0, TILES)):
             nc.scalar.activation(
-                out=inverse_root[b][:],
-                in_=square_sum[:],
+                out=inverse_root[b][:, tiles],
+                in_=square_sum[b][:, tiles],
                 func=ACT.Abs_reciprocal_sqrt,
                 bias=eps[:],
                 scale=1.0 / HIDDEN,
             )
 
-        def normalise(b):
-            x = normed.tile([P, TILES * HIDDEN], BF16, name="x")
-            for j in range(TILES):
-                nc.scalar.activation(
-                    out=x[:, j * HIDDEN : (j + 1) * HIDDEN],
-                    in_=gained_tokens[b][:, j, :],
-                    func=ACT.Copy,
-                    scale=inverse_root[b][:, j : j + 1],
-                )
-            return x
+        def normalise(b, j):
+            if j == 0:
+                x_rows[b] = normed.tile([P, TILES * HIDDEN], BF16, name="x")
+            nc.vector.scalar_tensor_tensor(
+                out=x_rows[b][:, j * HIDDEN : (j + 1) * HIDDEN],
+                in0=token_tiles[b][:, j, :],
+                scalar=inverse_root[b][:, j : j + 1],
+                in1=gain[:],
+                op0=ALU.mult,
+                op1=ALU.mult,
+            )
 
-        def k_to_partitions(row_words, grouped_words, copy):
-            for pair in range(TILES // 2):
-                flip = flipped.tile([P, 2, HALVES, P], F32, name="flip")
-                for i in range(2):
-                    for u in range(HALVES):
-                        nc.tensor.transpose(
-                            out=flip[:, i, u, :],
-                            in_=row_words[:, 2 * pair + i, u : HALVES * P : HALVES],
-                            identity=ident[:],
-                        )
-                copy(
-                    out=grouped_words[:, 2 * pair : 2 * pair + 2, :, :],
-                    in_=flip[:].rearrange("p i u n -> p i n u"),
-                )
+        def k_to_partitions(rows_2d, grouped_2d, pair, copy):
+            row_words = rows_2d.bitcast(F32).rearrange("p (i w) -> p i w", w=HALVES * P)
+            grouped_words = grouped_2d.bitcast(F32).rearrange("p (i n u) -> p i n u", n=P, u=HALVES)
+            flip = flipped.tile([P, 2, HALVES, P], F32, name="flip")
+            for i in range(2):
+                for u in range(HALVES):
+                    nc.tensor.transpose(
+                        out=flip[:, i, u, :],
+                        in_=row_words[:, 2 * pair + i, u : HALVES * P : HALVES],
+                        identity=ident[:],
+                    )
+            copy(
+                out=grouped_words[:, 2 * pair : 2 * pair + 2, :, :],
+                in_=flip[:].rearrange("p i u n -> p i n u"),
+            )
 
-        def as_row_words(tile_2d):
-            return tile_2d.bitcast(F32).rearrange("p (i w) -> p i w", i=TILES)
+        def flip_x(b, pair):
+            if pair == 0:
+                x_grouped[b] = normed.tile([P, QUANT], BF16, name="grouped", align_bytes=64)
+            k_to_partitions(x_rows[b][:], x_grouped[b][:], pair, nc.scalar.copy)
 
-        def as_grouped_words(tile_2d):
-            return tile_2d.bitcast(F32).rearrange("p (i n u) -> p i n u", i=TILES, u=HALVES)
-
-        def flip_x(x):
-            grouped = normed.tile([P, QUANT], BF16, name="grouped", align_bytes=64)
-            k_to_partitions(as_row_words(x[:]), as_grouped_words(grouped[:]), nc.scalar.copy)
-            return grouped
-
-        def quantise_x(b, grouped):
-            x_codes[b] = packed.tile([P, TILES * P], U32, name="x_codes", align_bytes=64)
-            x_scales[b] = packed.tile([P, TILES * P], U8, name="x_scales", align_bytes=64)
+        def quantise_x(b, first=0, tiles=TILES):
+            if first == 0:
+                x_codes[b] = packed.tile([P, TILES * P], U32, name="x_codes", align_bytes=64)
+                x_scales[b] = packed.tile([P, TILES * P], U8, name="x_scales", align_bytes=64)
+            rows = slice(first * P, (first + tiles) * P)
             nc.vector.quantize_mx(
-                out=x_codes[b][:].bitcast(FP8X4), scales=x_scales[b][:], in_=grouped[:]
+                out=x_codes[b][:, rows].bitcast(FP8X4),
+                scales=x_scales[b][:, rows],
+                in_=x_grouped[b][:, first * P * PACK : (first + tiles) * P * PACK],
             )
 
         w_grouped = const.tile([P, GROUPS * QUANT], BF16, align_bytes=64)
         w_codes = const.tile([P, COLUMNS], U32, align_bytes=64)
         w_scales = const.tile([P, COLUMNS], U8, align_bytes=64)
 
-        def pack_weights(g):
-            k_to_partitions(
-                as_row_words(w_raw[:, g * GROUP_HEADS * HIDDEN : (g + 1) * GROUP_HEADS * HIDDEN]),
-                as_grouped_words(w_grouped[:, g * QUANT : (g + 1) * QUANT]),
-                nc.vector.tensor_copy,
-            )
+        def flip_weights(g, pair, copy):
+            columns = slice(g * QUANT, (g + 1) * QUANT)
+            k_to_partitions(w_raw[:, columns], w_grouped[:, columns], pair, copy)
+
+        def quantise_weights(g):
             nc.vector.quantize_mx(
                 out=w_codes[:, g * GROUP : (g + 1) * GROUP].bitcast(FP8X4),
                 scales=w_scales[:, g * GROUP : (g + 1) * GROUP],
@@ -200,23 +200,34 @@ def tile_attentionlayerdecoder_pa_t_kernel(
         def by_head(columns):
             return columns.rearrange("p (h d) -> p h d", d=HEAD)
 
-        def multiply(b, g):
+        def multiply(b, m, by_scalar):
+            g, j = divmod(m, TILES)
             columns = slice(g * GROUP, (g + 1) * GROUP)
-            banks = []
-            for j in range(TILES):
-                rows = slice(j * P, (j + 1) * P)
-                acc = sums.tile([P, GROUP], F32, name="acc")
-                nc.tensor.matmul_mx(
-                    out=acc[:],
-                    lhsT=x_codes[b][:, rows].bitcast(FP8X4),
-                    lhsT_scale=x_scales[b][:, rows],
-                    rhs=w_codes[:, columns].bitcast(FP8X4),
-                    rhs_scale=w_scales[:, columns],
-                    start=True,
-                    stop=True,
-                )
-                banks.append(acc)
-            return banks
+            rows = slice(j * P, (j + 1) * P)
+            acc = sums.tile([P, GROUP], F32, name="acc")
+            nc.tensor.matmul_mx(
+                out=acc[:],
+                lhsT=x_codes[b][:, rows].bitcast(FP8X4),
+                lhsT_scale=x_scales[b][:, rows],
+                rhs=w_codes[:, columns].bitcast(FP8X4),
+                rhs_scale=w_scales[:, columns],
+                start=True,
+                stop=True,
+            )
+            if j == 0:
+                results_of[g] = results.tile([P, GROUP_HEADS, TILES, HEAD], F32, name="y")
+            y = results_of[g][:, :, j, :]
+            if by_scalar:
+                nc.scalar.copy(out=y, in_=by_head(acc[:]))
+                nc.gpsimd.tensor_tensor(out=y, in0=y, in1=by_head(bias[:, columns]), op=ALU.add)
+            else:
+                nc.vector.tensor_tensor(out=y, in0=by_head(acc[:]), in1=by_head(bias[:, columns]), op=ALU.add)
+            if j == TILES - 1:
+                if g < Q_GROUPS:
+                    store(q_out[b, g * GROUP_HEADS : (g + 1) * GROUP_HEADS], results_of[g][:])
+                else:
+                    store(k_out[b], results_of[g][:, 0:KV_HEADS])
+                    store(v_out[b], results_of[g][:, KV_HEADS : 2 * KV_HEADS])
 
         def store(heads_out, y_heads):
             nc.sync.dma_start(
@@ -224,56 +235,80 @@ def tile_attentionlayerdecoder_pa_t_kernel(
                 in_=y_heads.rearrange("p h j d -> p h (j d)"),
             )
 
-        def add_bias_and_store(b, g, banks):
-            columns = slice(g * GROUP, (g + 1) * GROUP)
-            y = results.tile([P, GROUP_HEADS, TILES, HEAD], F32, name="y")
-            for j in range(TILES):
-                if j == 0 and g < SCALAR_GROUPS:
-                    nc.scalar.copy(out=y[:, :, j, :], in_=by_head(banks[j][:]))
-                    nc.gpsimd.tensor_tensor(
-                        out=y[:, :, j, :], in0=y[:, :, j, :], in1=by_head(bias[:, columns]), op=ALU.add
-                    )
-                else:
-                    nc.vector.tensor_tensor(
-                        out=y[:, :, j, :],
-                        in0=by_head(banks[j][:]),
-                        in1=by_head(bias[:, columns]),
-                        op=ALU.add,
-                    )
-            if g < Q_GROUPS:
-                store(q_out[b, g * GROUP_HEADS : (g + 1) * GROUP_HEADS], y[:])
-            else:
-                store(k_out[b], y[:, 0:KV_HEADS])
-                store(v_out[b], y[:, KV_HEADS : 2 * KV_HEADS])
+        scalar_copy, vector_copy = nc.scalar.copy, nc.vector.tensor_copy
 
-        repeat_row(gain_row[:], gain[:])
-        for b in range(GAIN_AHEAD):
-            apply_gain(b, 0)
-            apply_gain(b, 1)
-        take_stats(0)
-        for g in range(GROUPS):
-            pack_weights(g)
-        for g in range(GROUPS):
-            repeat_row(bias_row[:, g * GROUP : (g + 1) * GROUP], bias[:, g * GROUP : (g + 1) * GROUP])
-        quantise_x(0, flip_x(normalise(0)))
-        take_stats(1)
+        square(0, 0)
+        square(0, 1)
+        root(0, slice(0, 2))
+        normalise(0, 0)
+        normalise(0, 1)
+        square(0, 2)
+        square(0, 3)
+        root(0, slice(2, 4))
+        normalise(0, 2)
+        normalise(0, 3)
+        flip_weights(0, 0, scalar_copy)
+        flip_weights(0, 1, scalar_copy)
+        flip_x(0, 0)
+        flip_x(0, 1)
+        quantise_weights(0)
+        repeat_bias(0, vector_copy)
+        quantise_x(0)
+        flip_weights(1, 0, vector_copy)
+        flip_weights(1, 1, scalar_copy)
+        multiply(0, 0, False)
+        square(1, 0)
+        multiply(0, 1, False)
+        square(1, 1)
+        quantise_weights(1)
+        square(1, 2)
+        multiply(0, 2, False)
+        square(1, 3)
+        root(1)
+        multiply(0, 3, False)
+        repeat_bias(1, scalar_copy)
+        flip_weights(2, 0, scalar_copy)
+        flip_weights(2, 1, vector_copy)
+        multiply(0, 4, False)
+        multiply(0, 5, True)
+        quantise_weights(2)
+        repeat_bias(2, scalar_copy)
+        multiply(0, 6, False)
+        multiply(0, 7, True)
+        normalise(1, 0)
+        square(2, 0)
+        normalise(1, 1)
+        square(2, 1)
+        multiply(0, 8, False)
+        multiply(0, 9, True)
+        normalise(1, 2)
+        square(2, 2)
+        normalise(1, 3)
+        square(2, 3)
+        root(2)
+        multiply(0, 10, False)
+        flip_x(1, 0)
+        flip_x(1, 1)
+        quantise_x(1)
+        multiply(0, 11, True)
 
-        for b in range(BATCHES):
+        for b in range(1, BATCHES):
             following = b + 1 < BATCHES
-            gain_due = b + GAIN_AHEAD < BATCHES
-            add_bias_and_store(b, 0, multiply(b, 0))
-            if gain_due:
-                apply_gain(b + GAIN_AHEAD, 0)
+            squares_due = b + 2 < BATCHES
+            for j in range(TILES):
+                multiply(b, 2 * j, False)
+                multiply(b, 2 * j + 1, True)
+                if following:
+                    normalise(b + 1, j)
+                if squares_due:
+                    square(b + 2, j)
+            if squares_due:
+                root(b + 2)
+            multiply(b, 8, False)
+            multiply(b, 9, False)
             if following:
-                x_next = normalise(b + 1)
-            banks = multiply(b, 1)
-            if following:
-                grouped_next = flip_x(x_next)
-            add_bias_and_store(b, 1, banks)
-            if gain_due:
-                apply_gain(b + GAIN_AHEAD, 1)
-            if following:
-                quantise_x(b + 1, grouped_next)
-            if b + 2 < BATCHES:
-                take_stats(b + 2)
-            add_bias_and_store(b, 2, multiply(b, 2))
+                flip_x(b + 1, 0)
+                flip_x(b + 1, 1)
+                quantise_x(b + 1)
+            multiply(b, 10, False)
+            multiply(b, 11, following)

@@ -30,6 +30,7 @@ GROUPS = COLUMNS // GROUP
 Q_GROUPS = Q_HEADS // GROUP_HEADS
 QUANT = TILES * P * PACK
 PASSES = GROUPS * TILES
+LEAD = 18
 
 FLOPS = 2 * BATCHES * TOKENS * HIDDEN * COLUMNS
 
@@ -41,14 +42,14 @@ def tile_attentionlayerdecoder_pa_t_kernel(
     with ExitStack() as ctx:
         ctx.enter_context(tc.manual_schedule())
         const = ctx.enter_context(tc.tile_pool(name="const", bufs=1))
-        stats = ctx.enter_context(tc.tile_pool(name="stats", bufs=3))
+        stats = ctx.enter_context(tc.tile_pool(name="stats", bufs=4))
         squares = ctx.enter_context(tc.tile_pool(name="squares", bufs=4))
-        normed = ctx.enter_context(tc.tile_pool(name="normed", bufs=2))
-        packed = ctx.enter_context(tc.tile_pool(name="packed", bufs=2))
+        normed = ctx.enter_context(tc.tile_pool(name="normed", bufs=3))
+        packed = ctx.enter_context(tc.tile_pool(name="packed", bufs=3))
         results = ctx.enter_context(tc.tile_pool(name="results", bufs=12))
         fixed = ctx.enter_context(tc.psum_pool(name="fixed", bufs=1))
-        flipped = ctx.enter_context(tc.psum_pool(name="flipped", bufs=2))
-        sums = ctx.enter_context(tc.psum_pool(name="sums", bufs=5))
+        flipped = ctx.enter_context(tc.psum_pool(name="flipped", bufs=3))
+        sums = ctx.enter_context(tc.psum_pool(name="sums", bufs=4))
 
         eps = const.tile([P, 1], F32)
         nc.vector.memset(eps[:], EPS)
@@ -107,6 +108,9 @@ def tile_attentionlayerdecoder_pa_t_kernel(
         gain = fixed.tile([P, HIDDEN], F32)
         nc.tensor.matmul(out=gain[:], lhsT=ones[:], rhs=gain_row[:], start=True, stop=True)
         bias = const.tile([P, COLUMNS], F32)
+        for unused in range(6):
+            idle = sums.tile([P, HIDDEN], F32, name="acc")
+            nc.tensor.matmul(out=idle[:], lhsT=ones[:], rhs=gain_row[:], start=True, stop=True)
 
         def repeat_bias(g, copy):
             columns = slice(g * GROUP, (g + 1) * GROUP)
@@ -292,23 +296,26 @@ def tile_attentionlayerdecoder_pa_t_kernel(
         quantise_x(1)
         multiply(0, 11, True)
 
+        def prepare(m):
+            for b in range(2, BATCHES):
+                lead, pace = (PASSES, 2) if b == 2 else (LEAD, 3)
+                since = m - (b * PASSES - lead)
+                if b > 2 and 0 <= since + 11 < 3 * TILES and (since + 11) % 3 == 1:
+                    square(b, (since + 11) // 3)
+                    if (since + 11) // 3 == TILES - 1:
+                        root(b)
+                if 0 <= since < pace * TILES and since % pace == 0:
+                    normalise(b, since // pace)
+                if since == (7 if pace == 3 else 5):
+                    flip_x(b, 0)
+                if since == (13 if pace == 3 else 8):
+                    flip_x(b, 1)
+                if m == (b - 1) * PASSES + 9:
+                    quantise_x(b)
+
+        for early in range(PASSES):
+            prepare(early)
         for b in range(1, BATCHES):
-            following = b + 1 < BATCHES
-            squares_due = b + 2 < BATCHES
-            for j in range(TILES):
-                multiply(b, 2 * j, False)
-                multiply(b, 2 * j + 1, True)
-                if following:
-                    normalise(b + 1, j)
-                if squares_due:
-                    square(b + 2, j)
-            if squares_due:
-                root(b + 2)
-            multiply(b, 8, False)
-            multiply(b, 9, False)
-            if following:
-                flip_x(b + 1, 0)
-                flip_x(b + 1, 1)
-                quantise_x(b + 1)
-            multiply(b, 10, False)
-            multiply(b, 11, following)
+            for m in range(PASSES):
+                multiply(b, m, (m % 3 == 1) if b == BATCHES - 1 else (m % 2 == 1 and m < PASSES - 1))
+                prepare(b * PASSES + m)

@@ -30,7 +30,7 @@ GROUPS = COLUMNS // GROUP
 Q_GROUPS = Q_HEADS // GROUP_HEADS
 QUANT = TILES * P * PACK
 PASSES = GROUPS * TILES
-LEAD = 18
+LEAD = 13
 
 FLOPS = 2 * BATCHES * TOKENS * HIDDEN * COLUMNS
 
@@ -277,38 +277,39 @@ def tile_attentionlayerdecoder_pa_t_kernel(
         multiply(0, 5, True)
         quantise_weights(2)
         repeat_bias(2, scalar_copy)
+        normalise(1, 0)
         multiply(0, 6, False)
         multiply(0, 7, True)
-        normalise(1, 0)
-        square(2, 0)
         normalise(1, 1)
+        square(2, 0)
+        normalise(1, 2)
         square(2, 1)
+        normalise(1, 3)
+        flip_x(1, 0)
         multiply(0, 8, False)
         multiply(0, 9, True)
-        normalise(1, 2)
+        flip_x(1, 1)
+        multiply(0, 10, False)
         square(2, 2)
-        normalise(1, 3)
+        quantise_x(1)
+        multiply(0, 11, False)
         square(2, 3)
         root(2)
-        multiply(0, 10, False)
-        flip_x(1, 0)
-        flip_x(1, 1)
-        quantise_x(1)
-        multiply(0, 11, True)
 
         def prepare(m):
             for b in range(2, BATCHES):
-                lead, pace = (PASSES, 2) if b == 2 else (LEAD, 3)
+                lead, pace = (PASSES, 2) if b == 2 else (LEAD, 2)
                 since = m - (b * PASSES - lead)
-                if b > 2 and 0 <= since + 11 < 3 * TILES and (since + 11) % 3 == 1:
-                    square(b, (since + 11) // 3)
-                    if (since + 11) // 3 == TILES - 1:
-                        root(b)
+                s = since + 7
+                if b > 2 and 0 <= s < 3 * TILES and s % 3 == 1:
+                    square(b, s // 3)
+                    if s // 3 % 2 == 1:
+                        root(b, slice(s // 3 - 1, s // 3 + 1))
                 if 0 <= since < pace * TILES and since % pace == 0:
                     normalise(b, since // pace)
-                if since == (7 if pace == 3 else 5):
+                if since == (5 if b > 2 else 5):
                     flip_x(b, 0)
-                if since == (13 if pace == 3 else 8):
+                if since == (9 if b > 2 else 8):
                     flip_x(b, 1)
                 if m == (b - 1) * PASSES + 9:
                     quantise_x(b)
@@ -317,5 +318,5 @@ def tile_attentionlayerdecoder_pa_t_kernel(
             prepare(early)
         for b in range(1, BATCHES):
             for m in range(PASSES):
-                multiply(b, m, (m % 3 == 1) if b == BATCHES - 1 else (m % 2 == 1 and m < PASSES - 1))
+                multiply(b, m, m in ((1, 4, 7, 10) if b == BATCHES - 1 else (0, 2, 5, 7, 10)))
                 prepare(b * PASSES + m)

@@ -31,6 +31,8 @@ Q_GROUPS = Q_HEADS // GROUP_HEADS
 QUANT = TILES * P * PACK
 PASSES = GROUPS * TILES
 LEAD = 13
+SCALAR_SHARE = 5
+LAST_SHARE = 4
 
 FLOPS = 2 * BATCHES * TOKENS * HIDDEN * COLUMNS
 
@@ -91,8 +93,8 @@ def tile_attentionlayerdecoder_pa_t_kernel(
         q_columns = Q_HEADS * HEAD
         kv_columns = KV_HEADS * HEAD
         first_half, second_half = load_tokens(0, pieces=2)
-        nc.sync.dma_start(out=gain_row[0:1, :], in_=norm_w.unsqueeze(0))
         load(first_half)
+        nc.sync.dma_start(out=gain_row[0:1, :], in_=norm_w.unsqueeze(0))
         load(second_half)
         load_weight_rows(0, Wq[0:GROUP, :])
         nc.sync.dma_start(out=bias_row[0:1, 0:q_columns], in_=bq.unsqueeze(0))
@@ -108,7 +110,7 @@ def tile_attentionlayerdecoder_pa_t_kernel(
         gain = fixed.tile([P, HIDDEN], F32)
         nc.tensor.matmul(out=gain[:], lhsT=ones[:], rhs=gain_row[:], start=True, stop=True)
         bias = const.tile([P, COLUMNS], F32)
-        for unused in range(6):
+        for unused in range(4):
             idle = sums.tile([P, HIDDEN], F32, name="acc")
             nc.tensor.matmul(out=idle[:], lhsT=ones[:], rhs=gain_row[:], start=True, stop=True)
 
@@ -298,25 +300,29 @@ def tile_attentionlayerdecoder_pa_t_kernel(
 
         def prepare(m):
             for b in range(2, BATCHES):
-                lead, pace = (PASSES, 2) if b == 2 else (LEAD, 2)
-                since = m - (b * PASSES - lead)
-                s = since + 7
-                if b > 2 and 0 <= s < 3 * TILES and s % 3 == 1:
-                    square(b, s // 3)
-                    if s // 3 % 2 == 1:
-                        root(b, slice(s // 3 - 1, s // 3 + 1))
-                if 0 <= since < pace * TILES and since % pace == 0:
-                    normalise(b, since // pace)
-                if since == (5 if b > 2 else 5):
+                since = m - (b * PASSES - LEAD)
+                j, rest = divmod(since + 10, 3)
+                if b > 2 and 0 <= j < TILES and rest == 0:
+                    square(b, j)
+                    if j == TILES - 1:
+                        root(b)
+                j, rest = divmod(since, 2)
+                if 0 <= j < TILES and rest == 0:
+                    normalise(b, j)
+                if since == 6:
                     flip_x(b, 0)
-                if since == (9 if b > 2 else 8):
+                if since == 9:
                     flip_x(b, 1)
-                if m == (b - 1) * PASSES + 9:
+                if since == 10:
                     quantise_x(b)
 
-        for early in range(PASSES):
-            prepare(early)
+        def evenly(share):
+            return [round(i * PASSES / share) for i in range(share)]
+
+        for m in range(PASSES):
+            prepare(m)
         for b in range(1, BATCHES):
+            by_scalar = evenly(LAST_SHARE if b == BATCHES - 1 else SCALAR_SHARE)
             for m in range(PASSES):
-                multiply(b, m, m in ((1, 4, 7, 10) if b == BATCHES - 1 else (0, 2, 5, 7, 10)))
+                multiply(b, m, m in by_scalar)
                 prepare(b * PASSES + m)

@@ -32,6 +32,8 @@ QUANT = TILES * P * PACK
 PASSES = GROUPS * TILES
 LEAD = 13
 SCALAR_SHARE = 5
+TWO_QUEUES_FROM = 5
+STORE_DELAY = 3
 LAST_SHARE = 4
 
 FLOPS = 2 * BATCHES * TOKENS * HIDDEN * COLUMNS
@@ -228,15 +230,27 @@ def tile_attentionlayerdecoder_pa_t_kernel(
                 nc.gpsimd.tensor_tensor(out=y, in0=y, in1=by_head(bias[:, columns]), op=ALU.add)
             else:
                 nc.vector.tensor_tensor(out=y, in0=by_head(acc[:]), in1=by_head(bias[:, columns]), op=ALU.add)
+            passes_done = b * PASSES + m
             if j == TILES - 1:
                 if g < Q_GROUPS:
-                    store(q_out[b, g * GROUP_HEADS : (g + 1) * GROUP_HEADS], results_of[g][:])
+                    first = q_out[b, g * GROUP_HEADS : g * GROUP_HEADS + 2]
+                    second = q_out[b, g * GROUP_HEADS + 2 : (g + 1) * GROUP_HEADS]
                 else:
-                    store(k_out[b], results_of[g][:, 0:KV_HEADS])
-                    store(v_out[b], results_of[g][:, KV_HEADS : 2 * KV_HEADS])
+                    first, second = k_out[b], v_out[b]
+                store(nc.sync, first, results_of[g][:, 0:2])
+                if b >= TWO_QUEUES_FROM:
+                    pending.append((passes_done + STORE_DELAY, second, results_of[g][:, 2:4]))
+                else:
+                    store(nc.sync, second, results_of[g][:, 2:4])
+            while pending and (pending[0][0] <= passes_done or passes_done == BATCHES * PASSES - 1):
+                due, heads_out, y_heads = pending[0]
+                pending.remove(pending[0])
+                store(nc.scalar, heads_out, y_heads)
 
-        def store(heads_out, y_heads):
-            nc.sync.dma_start(
+        pending = []
+
+        def store(engine, heads_out, y_heads):
+            engine.dma_start(
                 out=heads_out.rearrange("h (p j) d -> p h (j d)", j=TILES),
                 in_=y_heads.rearrange("p h j d -> p h (j d)"),
             )

from contextlib import ExitStack

import concourse.masks as masks
import concourse.mybir as mybir

F32 = mybir.dt.float32
BF16 = mybir.dt.bfloat16
U32 = mybir.dt.uint32
U8 = mybir.dt.uint8
FP8X4 = mybir.dt.float8_e4m3fn_x4
ACT = mybir.ActivationFunctionType
ALU = mybir.AluOpType

P = 128
BATCHES = 8
TOKENS = 512
HIDDEN = 512
HEAD = 128
Q_HEADS = 8
KV_HEADS = 2
EPS = 2.0**-23

TILES = TOKENS // P
PACK = 4
HALVES = 2
GROUP_HEADS = 4
GROUP = GROUP_HEADS * HEAD
COLUMNS = (Q_HEADS + 2 * KV_HEADS) * HEAD
GROUPS = COLUMNS // GROUP
Q_GROUPS = Q_HEADS // GROUP_HEADS
QUANT = TILES * P * PACK
PASSES = GROUPS * TILES
LEAD = 13
SCALAR_SHARE = 5
TWO_QUEUES_FROM = 5
STORE_DELAY = 3
LAST_SHARE = 4

FLOPS = 2 * BATCHES * TOKENS * HIDDEN * COLUMNS


def tile_attentionlayerdecoder_pa_t_kernel(
    tc, tokens, norm_w, Wq, bq, Wk, bk, Wv, bv, q_out, k_out, v_out
):
    nc = tc.nc
    with ExitStack() as ctx:
        ctx.enter_context(tc.manual_schedule())
        const = ctx.enter_context(tc.tile_pool(name="const", bufs=1))
        stats = ctx.enter_context(tc.tile_pool(name="stats", bufs=4))
        squares = ctx.enter_context(tc.tile_pool(name="squares", bufs=4))
        normed = ctx.enter_context(tc.tile_pool(name="normed", bufs=3))
        packed = ctx.enter_context(tc.tile_pool(name="packed", bufs=3))
        results = ctx.enter_context(tc.tile_pool(name="results", bufs=12))
        fixed = ctx.enter_context(tc.psum_pool(name="fixed", bufs=1))
        flipped = ctx.enter_context(tc.psum_pool(name="flipped", bufs=3))
        sums = ctx.enter_context(tc.psum_pool(name="sums", bufs=4))

        eps = const.tile([P, 1], F32)
        nc.vector.memset(eps[:], EPS)
        gain_row = const.tile([P, HIDDEN], BF16)
        nc.vector.memset(gain_row[:], 0.0)
        ones = const.tile([P, P], BF16)
        nc.vector.memset(ones[:], 1.0)
        ident = const.tile([P, P], F32)
        masks.make_identity(nc, ident[:])
        bias_row = const.tile([P, COLUMNS], BF16)
        nc.vector.memset(bias_row[:], 0.0)
        table_warm = const.tile([P, 1], F32)
        nc.scalar.activation(out=table_warm[:], in_=eps[:], func=ACT.Abs_reciprocal_sqrt)

        token_tiles = {}

        def load_tokens(b, pieces=1):
            token_tiles[b] = const.tile([P, TILES, HIDDEN], BF16, name="tokens%d" % b)
            rows = tokens[b].rearrange("(p j) k -> p j k", j=TILES)
            width = TILES // pieces
            return [
                (token_tiles[b][:, i * width : (i + 1) * width, :], rows[:, i * width : (i + 1) * width, :])
                for i in range(pieces)
            ]

        def load(piece):
            nc.sync.dma_start(out=piece[0], in_=piece[1])

        w_raw = const.tile([P, COLUMNS // P * HIDDEN], BF16)
        w_rows = w_raw[:].rearrange("p (r k) -> p r k", k=HIDDEN)

        def load_weight_rows(first_tile, rows):
            n_tiles = rows.shape[0] // P
            nc.sync.dma_start(
                out=w_rows[:, first_tile : first_tile + n_tiles, :],
                in_=rows.rearrange("(r p) k -> p r k", p=P),
            )

        q_columns = Q_HEADS * HEAD
        kv_columns = KV_HEADS * HEAD
        first_half, second_half = load_tokens(0, pieces=2)
        load(first_half)
        nc.sync.dma_start(out=gain_row[0:1, :], in_=norm_w.unsqueeze(0))
        load(second_half)
        load_weight_rows(0, Wq[0:GROUP, :])
        nc.sync.dma_start(out=bias_row[0:1, 0:q_columns], in_=bq.unsqueeze(0))
        nc.sync.dma_start(out=bias_row[0:1, q_columns : q_columns + kv_columns], in_=bk.unsqueeze(0))
        nc.sync.dma_start(out=bias_row[0:1, q_columns + kv_columns : COLUMNS], in_=bv.unsqueeze(0))
        load_weight_rows(GROUP_HEADS, Wq[GROUP : 2 * GROUP, :])
        load(load_tokens(1)[0])
        load_weight_rows(Q_HEADS, Wk)
        load_weight_rows(Q_HEADS + KV_HEADS, Wv)
        for b in range(2, BATCHES):
            load(load_tokens(b)[0])

        gain = fixed.tile([P, HIDDEN], F32)
        nc.tensor.matmul(out=gain[:], lhsT=ones[:], rhs=gain_row[:], start=True, stop=True)
        bias = const.tile([P, COLUMNS], F32)
        for unused in range(4):
            idle = sums.tile([P, HIDDEN], F32, name="acc")
            nc.tensor.matmul(out=idle[:], lhsT=ones[:], rhs=gain_row[:], start=True, stop=True)

        def repeat_bias(g, copy):
            columns = slice(g * GROUP, (g + 1) * GROUP)
            spread = sums.tile([P, GROUP], F32, name="acc")
            nc.tensor.matmul(out=spread[:], lhsT=ones[:], rhs=bias_row[:, columns], start=True, stop=True)
            copy(out=bias[:, columns], in_=spread[:])

        square_sum, inverse_root, x_rows, x_grouped = {}, {}, {}, {}
        x_codes, x_scales, results_of = {}, {}, {}

        def square(b, j):
            if j == 0:
                square_sum[b] = stats.tile([P, TILES], F32, name="square_sum")
                inverse_root[b] = stats.tile([P, TILES], F32, name="inverse_root")
            unread = squares.tile([P, HIDDEN], BF16, name="unread")
            nc.scalar.activation(
                out=unread[:],
                in_=token_tiles[b][:, j, :],
                func=ACT.Square,
                accum_out=square_sum[b][:, j : j + 1],
            )

        def root(b, tiles=slice(0, TILES)):
            nc.scalar.activation(
                out=inverse_root[b][:, tiles],
                in_=square_sum[b][:, tiles],
                func=ACT.Abs_reciprocal_sqrt,
                bias=eps[:],
                scale=1.0 / HIDDEN,
            )

        def normalise(b, j):
            if j == 0:
                x_rows[b] = normed.tile([P, TILES * HIDDEN], BF16, name="x")
            nc.vector.scalar_tensor_tensor(
                out=x_rows[b][:, j * HIDDEN : (j + 1) * HIDDEN],
                in0=token_tiles[b][:, j, :],
                scalar=inverse_root[b][:, j : j + 1],
                in1=gain[:],
                op0=ALU.mult,
                op1=ALU.mult,
            )

        def k_to_partitions(rows_2d, grouped_2d, pair, copy):
            row_words = rows_2d.bitcast(F32).rearrange("p (i w) -> p i w", w=HALVES * P)
            grouped_words = grouped_2d.bitcast(F32).rearrange("p (i n u) -> p i n u", n=P, u=HALVES)
            flip = flipped.tile([P, 2, HALVES, P], F32, name="flip")
            for i in range(2):
                for u in range(HALVES):
                    nc.tensor.transpose(
                        out=flip[:, i, u, :],
                        in_=row_words[:, 2 * pair + i, u : HALVES * P : HALVES],
                        identity=ident[:],
                    )
            copy(
                out=grouped_words[:, 2 * pair : 2 * pair + 2, :, :],
                in_=flip[:].rearrange("p i u n -> p i n u"),
            )

        def flip_x(b, pair):
            if pair == 0:
                x_grouped[b] = normed.tile([P, QUANT], BF16, name="grouped", align_bytes=64)
            k_to_partitions(x_rows[b][:], x_grouped[b][:], pair, nc.scalar.copy)

        def quantise_x(b, first=0, tiles=TILES):
            if first == 0:
                x_codes[b] = packed.tile([P, TILES * P], U32, name="x_codes", align_bytes=64)
                x_scales[b] = packed.tile([P, TILES * P], U8, name="x_scales", align_bytes=64)
            rows = slice(first * P, (first + tiles) * P)
            nc.vector.quantize_mx(
                out=x_codes[b][:, rows].bitcast(FP8X4),
                scales=x_scales[b][:, rows],
                in_=x_grouped[b][:, first * P * PACK : (first + tiles) * P * PACK],
            )

        w_grouped = const.tile([P, GROUPS * QUANT], BF16, align_bytes=64)
        w_codes = const.tile([P, COLUMNS], U32, align_bytes=64)
        w_scales = const.tile([P, COLUMNS], U8, align_bytes=64)

        def flip_weights(g, pair, copy):
            columns = slice(g * QUANT, (g + 1) * QUANT)
            k_to_partitions(w_raw[:, columns], w_grouped[:, columns], pair, copy)

        def quantise_weights(g):
            nc.vector.quantize_mx(
                out=w_codes[:, g * GROUP : (g + 1) * GROUP].bitcast(FP8X4),
                scales=w_scales[:, g * GROUP : (g + 1) * GROUP],
                in_=w_grouped[:, g * QUANT : (g + 1) * QUANT],
            )

        def by_head(columns):
            return columns.rearrange("p (h d) -> p h d", d=HEAD)

        def multiply(b, m, by_scalar):
            g, j = divmod(m, TILES)
            columns = slice(g * GROUP, (g + 1) * GROUP)
            rows = slice(j * P, (j + 1) * P)
            acc = sums.tile([P, GROUP], F32, name="acc")
            nc.tensor.matmul_mx(
                out=acc[:],
                lhsT=x_codes[b][:, rows].bitcast(FP8X4),
                lhsT_scale=x_scales[b][:, rows],
                rhs=w_codes[:, columns].bitcast(FP8X4),
                rhs_scale=w_scales[:, columns],
                start=True,
                stop=True,
            )
            if j == 0:
                results_of[g] = results.tile([P, GROUP_HEADS, TILES, HEAD], F32, name="y")
            y = results_of[g][:, :, j, :]
            if by_scalar:
                nc.scalar.copy(out=y, in_=by_head(acc[:]))
                nc.gpsimd.tensor_tensor(out=y, in0=y, in1=by_head(bias[:, columns]), op=ALU.add)
            else:
                nc.vector.tensor_tensor(out=y, in0=by_head(acc[:]), in1=by_head(bias[:, columns]), op=ALU.add)
            passes_done = b * PASSES + m
            if j == TILES - 1:
                if g < Q_GROUPS:
                    first = q_out[b, g * GROUP_HEADS : g * GROUP_HEADS + 2]
                    second = q_out[b, g * GROUP_HEADS + 2 : (g + 1) * GROUP_HEADS]
                else:
                    first, second = k_out[b], v_out[b]
                store(nc.sync, first, results_of[g][:, 0:2])
                if b >= TWO_QUEUES_FROM:
                    pending.append((passes_done + STORE_DELAY, second, results_of[g][:, 2:4]))
                else:
                    store(nc.sync, second, results_of[g][:, 2:4])
            while pending and (pending[0][0] <= passes_done or passes_done == BATCHES * PASSES - 1):
                due, heads_out, y_heads = pending[0]
                pending.remove(pending[0])
                store(nc.scalar, heads_out, y_heads)

        pending = []

        def store(engine, heads_out, y_heads):
            engine.dma_start(
                out=heads_out.rearrange("h (p j) d -> p h (j d)", j=TILES),
                in_=y_heads.rearrange("p h j d -> p h (j d)"),
            )

        scalar_copy, vector_copy = nc.scalar.copy, nc.vector.tensor_copy

        square(0, 0)
        square(0, 1)
        root(0, slice(0, 2))
        normalise(0, 0)
        normalise(0, 1)
        square(0, 2)
        square(0, 3)
        root(0, slice(2, 4))
        normalise(0, 2)
        normalise(0, 3)
        flip_weights(0, 0, scalar_copy)
        flip_weights(0, 1, scalar_copy)
        flip_x(0, 0)
        flip_x(0, 1)
        quantise_weights(0)
        repeat_bias(0, vector_copy)
        quantise_x(0)
        flip_weights(1, 0, vector_copy)
        flip_weights(1, 1, scalar_copy)
        multiply(0, 0, False)
        square(1, 0)
        multiply(0, 1, False)
        square(1, 1)
        quantise_weights(1)
        square(1, 2)
        multiply(0, 2, False)
        square(1, 3)
        root(1)
        multiply(0, 3, False)
        repeat_bias(1, scalar_copy)
        flip_weights(2, 0, scalar_copy)
        flip_weights(2, 1, vector_copy)
        multiply(0, 4, False)
        multiply(0, 5, True)
        quantise_weights(2)
        repeat_bias(2, scalar_copy)
        normalise(1, 0)
        multiply(0, 6, False)
        multiply(0, 7, True)
        normalise(1, 1)
        square(2, 0)
        normalise(1, 2)
        square(2, 1)
        normalise(1, 3)
        flip_x(1, 0)
        multiply(0, 8, False)
        multiply(0, 9, True)
        flip_x(1, 1)
        multiply(0, 10, False)
        square(2, 2)
        quantise_x(1)
        multiply(0, 11, False)
        square(2, 3)
        root(2)

        def prepare(m):
            for b in range(2, BATCHES):
                since = m - (b * PASSES - LEAD)
                j, rest = divmod(since + 10, 3)
                if b > 2 and 0 <= j < TILES and rest == 0:
                    square(b, j)
                    if j == TILES - 1:
                        root(b)
                j, rest = divmod(since, 2)
                if 0 <= j < TILES and rest == 0:
                    normalise(b, j)
                if since == 6:
                    flip_x(b, 0)
                if since == 9:
                    flip_x(b, 1)
                if since == 10:
                    quantise_x(b)

        def evenly(share):
            return [round(i * PASSES / share) for i in range(share)]

        for m in range(PASSES):
            prepare(m)
        for b in range(1, BATCHES):
            by_scalar = evenly(LAST_SHARE if b == BATCHES - 1 else SCALAR_SHARE)
            for m in range(PASSES):
                multiply(b, m, m in by_scalar)
                prepare(b * PASSES + m)
